import numpy as np
import ml_dtypes


def mxq(x, axis, fmt="e4m3"):
    dtype, down = {"e4m3": (ml_dtypes.float8_e4m3fn, 7), "e5m2": (ml_dtypes.float8_e5m2, 14)}[fmt]
    v = np.moveaxis(np.asarray(x, np.float32).astype(ml_dtypes.bfloat16).astype(np.float64), axis, -1)
    blocks = v.reshape(v.shape[:-1] + (-1, 32))
    amax = np.abs(blocks).max(-1, keepdims=True)
    byte = np.maximum(np.where(amax > 0, np.frexp(amax)[1] - 1 + 127, 0) - down, 1)
    scale = np.exp2(byte - 127.0)
    codes = (blocks / scale).astype(np.float32).astype(dtype).astype(np.float64)
    return np.moveaxis((codes * scale).reshape(v.shape), -1, axis)


WIDE = False


def mx_kscale(k):
    if not WIDE:
        return np.ones(k)
    levels = np.array([10, -10, 5, -5, 0])
    a = np.random.permutation(np.resize(levels, k // 512 * 4)).reshape(k // 512, 4)
    idx = np.arange(k)
    return np.exp2(a[idx // 512, idx % 128 // 32])


BF16 = ml_dtypes.bfloat16


def bf(x):
    return np.asarray(x, np.float32).astype(BF16)


def f64(x):
    return np.asarray(x).astype(np.float64)


E2M1 = np.array([0.0, 0.5, 1.0, 1.5, 2.0, 3.0, 4.0, 6.0, -0.0, -0.5, -1.0, -1.5, -2.0, -3.0, -4.0, -6.0])


def pack_weight(w, fmt):
    k, n = w.shape
    w = f64(bf(w)).reshape(k // 32, 32, n)
    amax = np.abs(w).max(1)
    if fmt == "e4m3":
        byte = np.frexp(amax)[1] - 1 + 127 - 7
    else:
        mant, ex = np.frexp(amax / 6.0)
        byte = np.where(mant > 0.5, ex, ex - 1) + 127
    byte = np.clip(np.where(amax > 0, byte, 1), 1, 254)
    scaled = (w * np.exp2(127.0 - byte)[:, None, :]).reshape(k, n).astype(np.float32)
    by_word = np.ascontiguousarray(scaled.reshape(k // 512, 128, 4, n).transpose(0, 1, 3, 2))
    if fmt == "e4m3":
        words = by_word.astype(ml_dtypes.float8_e4m3fn).view(np.uint8)
    else:
        c = by_word.astype(ml_dtypes.float4_e2m1fn).view(np.uint8) & 0xF
        words = c[..., 0::2] | (c[..., 1::2] << 4)
    return np.ascontiguousarray(words), np.ascontiguousarray(byte.astype(np.uint8).reshape(k // 512, 16, n))


def unpack_weight(words, scales, fmt):
    g, p, n, _ = words.shape
    if fmt == "e4m3":
        vals = np.ascontiguousarray(words).view(ml_dtypes.float8_e4m3fn).astype(np.float64)
    else:
        nib = np.empty((g, p, n, 4), np.uint8)
        nib[..., 0::2] = words & 0xF
        nib[..., 1::2] = words >> 4
        vals = E2M1[nib]
    vals = vals * np.repeat(np.exp2(scales.astype(np.float64) - 127.0), 8, axis=1)[..., None]
    return vals.transpose(0, 1, 3, 2).reshape(g * 512, n)

def pack4(w):
    words, scales = pack_weight(w, "e2m1")
    return words.reshape(words.shape[0], 128, -1), scales


def unpack4(words, scales):
    return unpack_weight(words.reshape(words.shape[0], 128, -1, 2), scales, "e2m1")


B, IN, H = 1024, 1024, 1024


def sigmoid(v):
    return 1.0 / (1.0 + np.exp(-v))


def setup_inputs():
    s = mx_kscale(IN)
    inp = bf(np.random.standard_normal((B, IN)) * s)
    state = bf(np.random.standard_normal((B, H)))
    c = bf(np.tanh(np.random.standard_normal((B, H))))
    W2_words, W2_scales = pack4(np.random.standard_normal((IN, H)) * 0.7 / np.sqrt(IN) / s[:, None])
    U2_words, U2_scales = pack4(np.random.standard_normal((H, H)) * 0.7 / np.sqrt(H))
    bias_gate = bf(np.random.standard_normal((1, H)) * 0.5)
    return {'input': inp,
            'state': state,
            'c': c,
            'W2_words': W2_words,
            'W2_scales': W2_scales,
            'U2_words': U2_words,
            'U2_scales': U2_scales,
            'bias_gate': bias_gate}


def reference(input, state, c, W2_words, W2_scales, U2_words, U2_scales, bias_gate):
    h = f64(state)
    wComp2 = mxq(f64(input), 1, 'e4m3') @ unpack4(W2_words, W2_scales)
    uComp2 = mxq(h, 1, 'e4m3') @ unpack4(U2_words, U2_scales)
    z = sigmoid(wComp2 + uComp2 + f64(bias_gate))
    return z * h + (1.0 - z) * f64(c)

@@ -1,0 +1,158 @@
+from contextlib import ExitStack
+
+import concourse.mybir as mybir
+from concourse.masks import make_identity
+
+F32 = mybir.dt.float32
+BF16 = mybir.dt.bfloat16
+I32 = mybir.dt.int32
+U32 = mybir.dt.uint32
+U8 = mybir.dt.uint8
+FP8X4 = mybir.dt.float8_e4m3fn_x4
+FP4X4 = mybir.dt.float4_e2m1fn_x4
+ALU = mybir.AluOpType
+ACT = mybir.ActivationFunctionType
+
+P = 128
+ROWS = 1024
+FEATURES = 1024
+HIDDEN = 1024
+ROW_TILES = ROWS // P
+K_PASS = 512
+PASSES = FEATURES // K_PASS
+GROUPS = 2 * PASSES
+N_HALF = 512
+HALVES = HIDDEN // N_HALF
+LOAD_TILES = 2
+
+FLOPS = 2 * ROWS * (2 * FEATURES) * HIDDEN
+
+
+def tile_grulrcell_pb_kernel(
+    tc, inp, state, c, W2_words, W2_scales, U2_words, U2_scales, bias_gate, out
+):
+    nc = tc.nc
+
+    inp_rows = inp.rearrange("(p j) k -> p j k", j=ROW_TILES)
+    state_rows = state.rearrange("(p j) k -> p j k", j=ROW_TILES)
+    c_rows = c.rearrange("(p j) h -> p j h", j=ROW_TILES)
+    out_rows = out.rearrange("(p j) h -> p j h", j=ROW_TILES)
+
+    with ExitStack() as stack:
+        keep = stack.enter_context(tc.tile_pool(name="keep", bufs=1))
+        work = stack.enter_context(tc.tile_pool(name="work", bufs=3))
+        psum_t = stack.enter_context(tc.psum_pool(name="psum_t", bufs=2))
+        psum_v = stack.enter_context(tc.psum_pool(name="psum_v", bufs=2))
+
+        inp_sb = keep.tile([P, ROW_TILES, FEATURES], BF16)
+        state_sb = keep.tile([P, ROW_TILES, FEATURES], BF16)
+        c_sb = keep.tile([P, ROW_TILES, HIDDEN], BF16)
+        w_words = keep.tile([P, GROUPS, 2 * HIDDEN], U8, align_bytes=64)
+        w_scales = keep.tile([P, GROUPS, HIDDEN], U8, align_bytes=64)
+        bias_row = keep.tile([P, HIDDEN], BF16)
+        bias_all = keep.tile([P, HIDDEN], F32)
+        ones = keep.tile([P, P], BF16)
+        ident = keep.tile([P, P], F32)
+        table_warm = keep.tile([P, 1], F32)
+
+        nc.vector.memset(w_scales[:].rearrange("p k n -> p (k n)").bitcast(I32), 0)
+        nc.vector.memset(table_warm[:], 0.0)
+        nc.vector.memset(bias_row[:], 0.0)
+        nc.vector.memset(ones[:], 1.0)
+        make_identity(nc, ident[:])
+        nc.scalar.activation(out=table_warm[:], in_=table_warm[:], func=ACT.Sigmoid)
+
+        def load_rows(dst, src, first):
+            tiles = slice(first, first + LOAD_TILES)
+            nc.sync.dma_start(out=dst[:, tiles, :], in_=src[:, tiles, :])
+
+        def load_scales(scales, first_group):
+            groups = slice(first_group, first_group + PASSES)
+            for quad in range(4):
+                nc.sync.dma_start(
+                    out=w_scales[32 * quad : 32 * quad + 4, groups, :].bitcast(I32),
+                    in_=scales[:, 4 * quad : 4 * quad + 4, :].rearrange("g r n -> r g n").bitcast(I32),
+                )
+
+        def load_words(words, first_group):
+            groups = slice(first_group, first_group + PASSES)
+            nc.sync.dma_start(
+                out=w_words[:, groups, :].bitcast(I32),
+                in_=words.rearrange("g p b -> p g b").bitcast(I32),
+            )
+
+        load_rows(inp_sb, inp_rows, 0)
+        load_scales(W2_scales, 0)
+        load_scales(U2_scales, PASSES)
+        load_words(W2_words, 0)
+        load_rows(state_sb, state_rows, 0)
+        load_words(U2_words, PASSES)
+        nc.sync.dma_start(out=bias_row[0:1, :], in_=bias_gate[:, :])
+        load_rows(c_sb, c_rows, 0)
+        for first in range(LOAD_TILES, ROW_TILES, LOAD_TILES):
+            load_rows(inp_sb, inp_rows, first)
+            load_rows(state_sb, state_rows, first)
+            load_rows(c_sb, c_rows, first)
+
+        for half in range(HALVES):
+            cols = slice(half * N_HALF, (half + 1) * N_HALF)
+            spread = psum_v.tile([P, N_HALF], F32, tag="v%d" % half)
+            nc.tensor.matmul(out=spread[:], lhsT=ones[:], rhs=bias_row[:, cols], start=True, stop=True)
+            nc.scalar.copy(out=bias_all[:, cols], in_=spread[:])
+
+        for j in range(ROW_TILES):
+            grouped = work.tile([P, 2, PASSES, P, 4], BF16, align_bytes=64)
+            for operand, rows_sb in enumerate((inp_sb, state_sb)):
+                words = rows_sb[:, j, :].bitcast(F32)
+                flipped = psum_t.tile([P, PASSES, 2, P], F32, tag="flipped%d" % operand)
+                for g in range(PASSES):
+                    for u in range(2):
+                        nc.tensor.transpose(
+                            flipped[:, g, u, :],
+                            words[:, 256 * g + u : 256 * (g + 1) : 2],
+                            ident[:],
+                        )
+                nc.scalar.copy(
+                    out=grouped[:, operand]
+                    .rearrange("p g r t -> p (g r t)")
+                    .bitcast(F32)
+                    .rearrange("p (g r u) -> p g r u", g=PASSES, u=2),
+                    in_=flipped[:].rearrange("p g u r -> p g r u"),
+                )
+
+            codes = work.tile([P, GROUPS * P], U32, align_bytes=64)
+            code_scales = work.tile([P, GROUPS * P], U8, align_bytes=64)
+            nc.vector.quantize_mx(
+                out=codes[:].bitcast(FP8X4),
+                scales=code_scales[:],
+                in_=grouped[:].rearrange("p o g r t -> p (o g r t)"),
+            )
+
+            sums = [
+                psum_v.tile([P, N_HALF], F32, name="sums%d" % half, tag="v%d" % half)
+                for half in range(HALVES)
+            ]
+            for group in range(GROUPS):
+                rows = slice(group * P, (group + 1) * P)
+                for half in range(HALVES):
+                    nc.tensor.matmul_mx(
+                        out=sums[half][:],
+                        lhsT=codes[:, rows].bitcast(FP8X4),
+                        lhsT_scale=code_scales[:, rows],
+                        rhs=w_words[:, group, 2 * half * N_HALF : 2 * (half + 1) * N_HALF].bitcast(FP4X4),
+                        rhs_scale=w_scales[:, group, half * N_HALF : (half + 1) * N_HALF],
+                        start=(group == 0),
+                        stop=(group == GROUPS - 1),
+                    )
+
+            gate = work.tile([P, HIDDEN], F32)
+            for half in range(HALVES):
+                cols = slice(half * N_HALF, (half + 1) * N_HALF)
+                nc.vector.tensor_tensor(out=gate[:, cols], in0=sums[half][:], in1=bias_all[:, cols], op=ALU.add)
+            nc.scalar.activation(out=gate[:], in_=gate[:], func=ACT.Sigmoid)
+            diff = work.tile([P, HIDDEN], F32)
+            nc.vector.tensor_tensor(out=diff[:], in0=state_sb[:, j, :], in1=c_sb[:, j, :], op=ALU.subtract)
+            nc.vector.tensor_tensor(out=diff[:], in0=gate[:], in1=diff[:], op=ALU.mult)
+            result = work.tile([P, HIDDEN], F32)
+            nc.vector.tensor_tensor(out=result[:], in0=diff[:], in1=c_sb[:, j, :], op=ALU.add)
+            nc.sync.dma_start(out=out_rows[:, j, :], in_=result[:])

@@ -41,8 +41,10 @@ def tile_grulrcell_pb_kernel(
     with ExitStack() as stack:
         keep = stack.enter_context(tc.tile_pool(name="keep", bufs=1))
         work = stack.enter_context(tc.tile_pool(name="work", bufs=3))
-        psum_t = stack.enter_context(tc.psum_pool(name="psum_t", bufs=2))
-        psum_v = stack.enter_context(tc.psum_pool(name="psum_v", bufs=2))
+        psum_t = stack.enter_context(tc.psum_pool(name="psum_t", bufs=1))
+        psum_v = stack.enter_context(tc.psum_pool(name="psum_v", bufs=3))
+        psum_c = stack.enter_context(tc.psum_pool(name="psum_c", bufs=3))
+        stack.enter_context(tc.manual_schedule())
 
         inp_sb = keep.tile([P, ROW_TILES, FEATURES], BF16)
         state_sb = keep.tile([P, ROW_TILES, FEATURES], BF16)
@@ -53,17 +55,19 @@ def tile_grulrcell_pb_kernel(
         bias_all = keep.tile([P, HIDDEN], F32)
         ones = keep.tile([P, P], BF16)
         ident = keep.tile([P, P], F32)
+        ident_bf = keep.tile([P, P], BF16)
         table_warm = keep.tile([P, 1], F32)
 
         nc.vector.memset(w_scales[:].rearrange("p k n -> p (k n)").bitcast(I32), 0)
-        nc.vector.memset(table_warm[:], 0.0)
         nc.vector.memset(bias_row[:], 0.0)
+        nc.vector.memset(table_warm[:], 0.0)
         nc.vector.memset(ones[:], 1.0)
         make_identity(nc, ident[:])
+        make_identity(nc, ident_bf[:])
         nc.scalar.activation(out=table_warm[:], in_=table_warm[:], func=ACT.Sigmoid)
 
-        def load_rows(dst, src, first):
-            tiles = slice(first, first + LOAD_TILES)
+        def load_rows(dst, src, first, count):
+            tiles = slice(first, first + count)
             nc.sync.dma_start(out=dst[:, tiles, :], in_=src[:, tiles, :])
 
         def load_scales(scales, first_group):
@@ -81,27 +85,32 @@ def tile_grulrcell_pb_kernel(
                 in_=words.rearrange("g p b -> p g b").bitcast(I32),
             )
 
-        load_rows(inp_sb, inp_rows, 0)
+        nc.gpsimd.dma_start(out=bias_row[0:1, :], in_=bias_gate[:, :])
+        load_rows(inp_sb, inp_rows, 0, 1)
+        load_rows(state_sb, state_rows, 0, 1)
+        load_words(W2_words, 0)
+        load_words(U2_words, PASSES)
         load_scales(W2_scales, 0)
         load_scales(U2_scales, PASSES)
-        load_words(W2_words, 0)
-        load_rows(state_sb, state_rows, 0)
-        load_words(U2_words, PASSES)
-        nc.sync.dma_start(out=bias_row[0:1, :], in_=bias_gate[:, :])
-        load_rows(c_sb, c_rows, 0)
+        load_rows(c_sb, c_rows, 0, 1)
+        load_rows(inp_sb, inp_rows, 1, 1)
+        load_rows(state_sb, state_rows, 1, 1)
+        load_rows(c_sb, c_rows, 1, 1)
         for first in range(LOAD_TILES, ROW_TILES, LOAD_TILES):
-            load_rows(inp_sb, inp_rows, first)
-            load_rows(state_sb, state_rows, first)
-            load_rows(c_sb, c_rows, first)
+            load_rows(inp_sb, inp_rows, first, LOAD_TILES)
+            load_rows(state_sb, state_rows, first, LOAD_TILES)
+            load_rows(c_sb, c_rows, first, LOAD_TILES)
 
-        for half in range(HALVES):
-            cols = slice(half * N_HALF, (half + 1) * N_HALF)
-            spread = psum_v.tile([P, N_HALF], F32, tag="v%d" % half)
-            nc.tensor.matmul(out=spread[:], lhsT=ones[:], rhs=bias_row[:, cols], start=True, stop=True)
-            nc.scalar.copy(out=bias_all[:, cols], in_=spread[:])
+        grouped = {}
+        codes = {}
+        code_scales = {}
+        sums = {}
+        cand = {}
+        gate = {}
+        diff = {}
 
-        for j in range(ROW_TILES):
-            grouped = work.tile([P, 2, PASSES, P, 4], BF16, align_bytes=64)
+        def flip(j):
+            grouped[j] = work.tile([P, 2, PASSES, P, 4], BF16, name="grouped", align_bytes=64)
             for operand, rows_sb in enumerate((inp_sb, state_sb)):
                 words = rows_sb[:, j, :].bitcast(F32)
                 flipped = psum_t.tile([P, PASSES, 2, P], F32, tag="flipped%d" % operand)
@@ -113,46 +122,89 @@ def tile_grulrcell_pb_kernel(
                             ident[:],
                         )
                 nc.scalar.copy(
-                    out=grouped[:, operand]
+                    out=grouped[j][:, operand]
                     .rearrange("p g r t -> p (g r t)")
                     .bitcast(F32)
                     .rearrange("p (g r u) -> p g r u", g=PASSES, u=2),
                     in_=flipped[:].rearrange("p g u r -> p g r u"),
                 )
 
-            codes = work.tile([P, GROUPS * P], U32, align_bytes=64)
-            code_scales = work.tile([P, GROUPS * P], U8, align_bytes=64)
+        def quantise(j):
+            codes[j] = work.tile([P, GROUPS * P], U32, name="codes", align_bytes=64)
+            code_scales[j] = work.tile([P, GROUPS * P], U8, name="code_scales", align_bytes=64)
             nc.vector.quantize_mx(
-                out=codes[:].bitcast(FP8X4),
-                scales=code_scales[:],
-                in_=grouped[:].rearrange("p o g r t -> p (o g r t)"),
+                out=codes[j][:].bitcast(FP8X4),
+                scales=code_scales[j][:],
+                in_=grouped[j][:].rearrange("p o g r t -> p (o g r t)"),
             )
 
-            sums = [
-                psum_v.tile([P, N_HALF], F32, name="sums%d" % half, tag="v%d" % half)
-                for half in range(HALVES)
-            ]
+        def products(j):
+            sums[j] = [psum_v.tile([P, N_HALF], F32, name="sums") for half in range(HALVES)]
             for group in range(GROUPS):
                 rows = slice(group * P, (group + 1) * P)
                 for half in range(HALVES):
                     nc.tensor.matmul_mx(
-                        out=sums[half][:],
-                        lhsT=codes[:, rows].bitcast(FP8X4),
-                        lhsT_scale=code_scales[:, rows],
+                        out=sums[j][half][:],
+                        lhsT=codes[j][:, rows].bitcast(FP8X4),
+                        lhsT_scale=code_scales[j][:, rows],
                         rhs=w_words[:, group, 2 * half * N_HALF : 2 * (half + 1) * N_HALF].bitcast(FP4X4),
                         rhs_scale=w_scales[:, group, half * N_HALF : (half + 1) * N_HALF],
                         start=(group == 0),
                         stop=(group == GROUPS - 1),
                     )
 
-            gate = work.tile([P, HIDDEN], F32)
+        def candidate(j):
+            cand[j] = psum_c.tile([P, HIDDEN], BF16, name="cand")
             for half in range(HALVES):
                 cols = slice(half * N_HALF, (half + 1) * N_HALF)
-                nc.vector.tensor_tensor(out=gate[:, cols], in0=sums[half][:], in1=bias_all[:, cols], op=ALU.add)
-            nc.scalar.activation(out=gate[:], in_=gate[:], func=ACT.Sigmoid)
-            diff = work.tile([P, HIDDEN], F32)
-            nc.vector.tensor_tensor(out=diff[:], in0=state_sb[:, j, :], in1=c_sb[:, j, :], op=ALU.subtract)
-            nc.vector.tensor_tensor(out=diff[:], in0=gate[:], in1=diff[:], op=ALU.mult)
+                nc.tensor.matmul(out=cand[j][:, cols], lhsT=ident_bf[:], rhs=c_sb[:, j, cols], start=True, stop=True)
+
+        half_cols = [slice(half * N_HALF, (half + 1) * N_HALF) for half in range(HALVES)]
+
+        def add_bias(j):
+            gate[j] = work.tile([P, HIDDEN], F32, name="gate")
+            for half, cols in enumerate(half_cols):
+                nc.vector.tensor_tensor(out=gate[j][:, cols], in0=sums[j][half][:], in1=bias_all[:, cols], op=ALU.add)
+
+        def sigmoid(j):
+            for cols in half_cols:
+                nc.scalar.activation(out=gate[j][:, cols], in_=gate[j][:, cols], func=ACT.Sigmoid)
+
+        def difference(j):
+            diff[j] = work.tile([P, HIDDEN], F32, name="diff")
+            for cols in half_cols:
+                nc.vector.tensor_tensor(out=diff[j][:, cols], in0=state_sb[:, j, cols], in1=cand[j][:, cols], op=ALU.subtract)
+
+        def scale(j):
+            for cols in half_cols:
+                nc.gpsimd.tensor_tensor(out=diff[j][:, cols], in0=gate[j][:, cols], in1=diff[j][:, cols], op=ALU.mult)
+
+        def finish(j):
             result = work.tile([P, HIDDEN], F32)
-            nc.vector.tensor_tensor(out=result[:], in0=diff[:], in1=c_sb[:, j, :], op=ALU.add)
+            for cols in half_cols:
+                nc.vector.tensor_tensor(out=result[:, cols], in0=diff[j][:, cols], in1=cand[j][:, cols], op=ALU.add)
             nc.sync.dma_start(out=out_rows[:, j, :], in_=result[:])
+
+        flip(0)
+        quantise(0)
+        flip(1)
+        quantise(1)
+        for cols in half_cols:
+            spread = psum_v.tile([P, N_HALF], F32, tag="sums")
+            nc.tensor.matmul(out=spread[:], lhsT=ones[:], rhs=bias_row[:, cols], start=True, stop=True)
+            nc.scalar.copy(out=bias_all[:, cols], in_=spread[:])
+
+        for j in range(ROW_TILES):
+            products(j)
+            candidate(j)
+            if j + 2 < ROW_TILES:
+                flip(j + 2)
+            add_bias(j)
+            sigmoid(j)
+            difference(j)
+            if j + 2 < ROW_TILES:
+                quantise(j + 2)
+            scale(j)
+            if j >= 1:
+                finish(j - 1)
+        finish(ROW_TILES - 1)

@@ -23,7 +23,7 @@ PASSES = FEATURES // K_PASS
 GROUPS = 2 * PASSES
 N_HALF = 512
 HALVES = HIDDEN // N_HALF
-LOAD_TILES = 2
+C_LAG = 2
 
 FLOPS = 2 * ROWS * (2 * FEATURES) * HIDDEN
 
@@ -66,9 +66,8 @@ def tile_grulrcell_pb_kernel(
         make_identity(nc, ident_bf[:])
         nc.scalar.activation(out=table_warm[:], in_=table_warm[:], func=ACT.Sigmoid)
 
-        def load_rows(dst, src, first, count):
-            tiles = slice(first, first + count)
-            nc.sync.dma_start(out=dst[:, tiles, :], in_=src[:, tiles, :])
+        def load_rows(dst, src, j):
+            nc.sync.dma_start(out=dst[:, j, :], in_=src[:, j, :])
 
         def load_scales(scales, first_group):
             groups = slice(first_group, first_group + PASSES)
@@ -86,20 +85,19 @@ def tile_grulrcell_pb_kernel(
             )
 
         nc.gpsimd.dma_start(out=bias_row[0:1, :], in_=bias_gate[:, :])
-        load_rows(inp_sb, inp_rows, 0, 1)
-        load_rows(state_sb, state_rows, 0, 1)
-        load_words(W2_words, 0)
-        load_words(U2_words, PASSES)
+        load_rows(inp_sb, inp_rows, 0)
+        load_rows(state_sb, state_rows, 0)
         load_scales(W2_scales, 0)
+        load_words(W2_words, 0)
+        load_rows(inp_sb, inp_rows, 1)
+        load_rows(state_sb, state_rows, 1)
         load_scales(U2_scales, PASSES)
-        load_rows(c_sb, c_rows, 0, 1)
-        load_rows(inp_sb, inp_rows, 1, 1)
-        load_rows(state_sb, state_rows, 1, 1)
-        load_rows(c_sb, c_rows, 1, 1)
-        for first in range(LOAD_TILES, ROW_TILES, LOAD_TILES):
-            load_rows(inp_sb, inp_rows, first, LOAD_TILES)
-            load_rows(state_sb, state_rows, first, LOAD_TILES)
-            load_rows(c_sb, c_rows, first, LOAD_TILES)
+        load_words(U2_words, PASSES)
+        for j in range(C_LAG, ROW_TILES + C_LAG):
+            load_rows(c_sb, c_rows, j - C_LAG)
+            if j < ROW_TILES:
+                load_rows(inp_sb, inp_rows, j)
+                load_rows(state_sb, state_rows, j)
 
         grouped = {}
         codes = {}
@@ -194,16 +192,18 @@ def tile_grulrcell_pb_kernel(
             nc.tensor.matmul(out=spread[:], lhsT=ones[:], rhs=bias_row[:, cols], start=True, stop=True)
             nc.scalar.copy(out=bias_all[:, cols], in_=spread[:])
 
+        flipped_tiles = 2
         for j in range(ROW_TILES):
             products(j)
             candidate(j)
-            if j + 2 < ROW_TILES:
-                flip(j + 2)
             add_bias(j)
             sigmoid(j)
-            difference(j)
+            for ahead in range(flipped_tiles, min(j + 4, ROW_TILES)):
+                flip(ahead)
+            flipped_tiles = min(j + 4, ROW_TILES)
             if j + 2 < ROW_TILES:
                 quantise(j + 2)
+            difference(j)
             scale(j)
             if j >= 1:
                 finish(j - 1)

@@ -23,7 +23,6 @@ PASSES = FEATURES // K_PASS
 GROUPS = 2 * PASSES
 N_HALF = 512
 HALVES = HIDDEN // N_HALF
-C_LAG = 2
 
 FLOPS = 2 * ROWS * (2 * FEATURES) * HIDDEN
 
@@ -93,11 +92,12 @@ def tile_grulrcell_pb_kernel(
         load_rows(state_sb, state_rows, 1)
         load_scales(U2_scales, PASSES)
         load_words(U2_words, PASSES)
-        for j in range(C_LAG, ROW_TILES + C_LAG):
-            load_rows(c_sb, c_rows, j - C_LAG)
-            if j < ROW_TILES:
-                load_rows(inp_sb, inp_rows, j)
-                load_rows(state_sb, state_rows, j)
+        load_rows(c_sb, c_rows, 0)
+        load_rows(c_sb, c_rows, 1)
+        for j in range(2, ROW_TILES):
+            load_rows(inp_sb, inp_rows, j)
+            load_rows(state_sb, state_rows, j)
+            load_rows(c_sb, c_rows, j)
 
         grouped = {}
         codes = {}
@@ -138,9 +138,9 @@ def tile_grulrcell_pb_kernel(
 
         def products(j):
             sums[j] = [psum_v.tile([P, N_HALF], F32, name="sums") for half in range(HALVES)]
-            for group in range(GROUPS):
-                rows = slice(group * P, (group + 1) * P)
-                for half in range(HALVES):
+            for half in range(HALVES):
+                for group in range(GROUPS):
+                    rows = slice(group * P, (group + 1) * P)
                     nc.tensor.matmul_mx(
                         out=sums[j][half][:],
                         lhsT=codes[j][:, rows].bitcast(FP8X4),
@@ -181,29 +181,32 @@ def tile_grulrcell_pb_kernel(
             result = work.tile([P, HIDDEN], F32)
             for cols in half_cols:
                 nc.vector.tensor_tensor(out=result[:, cols], in0=diff[j][:, cols], in1=cand[j][:, cols], op=ALU.add)
-            nc.sync.dma_start(out=out_rows[:, j, :], in_=result[:])
+                nc.sync.dma_start(out=out_rows[:, j, cols], in_=result[:, cols])
 
         flip(0)
         quantise(0)
         flip(1)
-        quantise(1)
         for cols in half_cols:
             spread = psum_v.tile([P, N_HALF], F32, tag="sums")
             nc.tensor.matmul(out=spread[:], lhsT=ones[:], rhs=bias_row[:, cols], start=True, stop=True)
             nc.scalar.copy(out=bias_all[:, cols], in_=spread[:])
 
-        flipped_tiles = 2
         for j in range(ROW_TILES):
+            if j + 1 < ROW_TILES:
+                quantise(j + 1)
             products(j)
-            candidate(j)
+            if j == 0:
+                candidate(0)
+            if j + 1 < ROW_TILES:
+                candidate(j + 1)
             add_bias(j)
             sigmoid(j)
-            for ahead in range(flipped_tiles, min(j + 4, ROW_TILES)):
-                flip(ahead)
-            flipped_tiles = min(j + 4, ROW_TILES)
             if j + 2 < ROW_TILES:
-                quantise(j + 2)
-            difference(j)
+                flip(j + 2)
+            if j == 0:
+                difference(0)
+            if j + 1 < ROW_TILES:
+                difference(j + 1)
             scale(j)
             if j >= 1:
                 finish(j - 1)

@@ -39,7 +39,7 @@ def tile_grulrcell_pb_kernel(
 
     with ExitStack() as stack:
         keep = stack.enter_context(tc.tile_pool(name="keep", bufs=1))
-        work = stack.enter_context(tc.tile_pool(name="work", bufs=3))
+        work = stack.enter_context(tc.tile_pool(name="work", bufs=4))
         psum_t = stack.enter_context(tc.psum_pool(name="psum_t", bufs=1))
         psum_v = stack.enter_context(tc.psum_pool(name="psum_v", bufs=3))
         psum_c = stack.enter_context(tc.psum_pool(name="psum_c", bufs=3))
@@ -190,24 +190,26 @@ def tile_grulrcell_pb_kernel(
             spread = psum_v.tile([P, N_HALF], F32, tag="sums")
             nc.tensor.matmul(out=spread[:], lhsT=ones[:], rhs=bias_row[:, cols], start=True, stop=True)
             nc.scalar.copy(out=bias_all[:, cols], in_=spread[:])
+        quantise(1)
+        products(0)
+        candidate(0)
+        flip(2)
 
         for j in range(ROW_TILES):
-            if j + 1 < ROW_TILES:
-                quantise(j + 1)
-            products(j)
-            if j == 0:
-                candidate(0)
-            if j + 1 < ROW_TILES:
-                candidate(j + 1)
             add_bias(j)
             sigmoid(j)
             if j + 2 < ROW_TILES:
-                flip(j + 2)
+                quantise(j + 2)
+            if j + 1 < ROW_TILES:
+                candidate(j + 1)
+                products(j + 1)
+            if j + 3 < ROW_TILES:
+                flip(j + 3)
+            if j >= 1:
+                finish(j - 1)
             if j == 0:
                 difference(0)
             if j + 1 < ROW_TILES:
                 difference(j + 1)
             scale(j)
-            if j >= 1:
-                finish(j - 1)
         finish(ROW_TILES - 1)

@@ -88,16 +88,19 @@ def tile_grulrcell_pb_kernel(
         load_rows(state_sb, state_rows, 0)
         load_scales(W2_scales, 0)
         load_words(W2_words, 0)
+        load_words(U2_words, PASSES)
+        load_scales(U2_scales, PASSES)
         load_rows(inp_sb, inp_rows, 1)
         load_rows(state_sb, state_rows, 1)
-        load_scales(U2_scales, PASSES)
-        load_words(U2_words, PASSES)
         load_rows(c_sb, c_rows, 0)
         load_rows(c_sb, c_rows, 1)
-        for j in range(2, ROW_TILES):
+        load_rows(inp_sb, inp_rows, 2)
+        load_rows(state_sb, state_rows, 2)
+        for j in range(3, ROW_TILES):
             load_rows(inp_sb, inp_rows, j)
             load_rows(state_sb, state_rows, j)
-            load_rows(c_sb, c_rows, j)
+            load_rows(c_sb, c_rows, j - 1)
+        load_rows(c_sb, c_rows, ROW_TILES - 1)
 
         grouped = {}
         codes = {}
@@ -119,7 +122,8 @@ def tile_grulrcell_pb_kernel(
                             words[:, 256 * g + u : 256 * (g + 1) : 2],
                             ident[:],
                         )
-                nc.scalar.copy(
+                copy = nc.vector.tensor_copy if operand == 1 and j < 2 else nc.scalar.copy
+                copy(
                     out=grouped[j][:, operand]
                     .rearrange("p g r t -> p (g r t)")
                     .bitcast(F32)
@@ -127,29 +131,30 @@ def tile_grulrcell_pb_kernel(
                     in_=flipped[:].rearrange("p g u r -> p g r u"),
                 )
 
-        def quantise(j):
-            codes[j] = work.tile([P, GROUPS * P], U32, name="codes", align_bytes=64)
-            code_scales[j] = work.tile([P, GROUPS * P], U8, name="code_scales", align_bytes=64)
+        def quantise(j, operands=(0, 1)):
+            if operands[0] == 0:
+                codes[j] = work.tile([P, GROUPS * P], U32, name="codes", align_bytes=64)
+                code_scales[j] = work.tile([P, GROUPS * P], U8, name="code_scales", align_bytes=64)
+            cols = slice(operands[0] * PASSES * P, (operands[-1] + 1) * PASSES * P)
             nc.vector.quantize_mx(
-                out=codes[j][:].bitcast(FP8X4),
-                scales=code_scales[j][:],
-                in_=grouped[j][:].rearrange("p o g r t -> p (o g r t)"),
+                out=codes[j][:, cols].bitcast(FP8X4),
+                scales=code_scales[j][:, cols],
+                in_=grouped[j][:, operands[0] : operands[-1] + 1].rearrange("p o g r t -> p (o g r t)"),
             )
 
-        def products(j):
+        def products(j, order=None):
             sums[j] = [psum_v.tile([P, N_HALF], F32, name="sums") for half in range(HALVES)]
-            for half in range(HALVES):
-                for group in range(GROUPS):
-                    rows = slice(group * P, (group + 1) * P)
-                    nc.tensor.matmul_mx(
-                        out=sums[j][half][:],
-                        lhsT=codes[j][:, rows].bitcast(FP8X4),
-                        lhsT_scale=code_scales[j][:, rows],
-                        rhs=w_words[:, group, 2 * half * N_HALF : 2 * (half + 1) * N_HALF].bitcast(FP4X4),
-                        rhs_scale=w_scales[:, group, half * N_HALF : (half + 1) * N_HALF],
-                        start=(group == 0),
-                        stop=(group == GROUPS - 1),
-                    )
+            for half, group in order or [(half, group) for half in range(HALVES) for group in range(GROUPS)]:
+                rows = slice(group * P, (group + 1) * P)
+                nc.tensor.matmul_mx(
+                    out=sums[j][half][:],
+                    lhsT=codes[j][:, rows].bitcast(FP8X4),
+                    lhsT_scale=code_scales[j][:, rows],
+                    rhs=w_words[:, group, 2 * half * N_HALF : 2 * (half + 1) * N_HALF].bitcast(FP4X4),
+                    rhs_scale=w_scales[:, group, half * N_HALF : (half + 1) * N_HALF],
+                    start=(group == 0),
+                    stop=(group == GROUPS - 1),
+                )
 
         def candidate(j):
             cand[j] = psum_c.tile([P, HIDDEN], BF16, name="cand")
@@ -184,18 +189,28 @@ def tile_grulrcell_pb_kernel(
                 nc.sync.dma_start(out=out_rows[:, j, cols], in_=result[:, cols])
 
         flip(0)
-        quantise(0)
-        flip(1)
         for cols in half_cols:
             spread = psum_v.tile([P, N_HALF], F32, tag="sums")
             nc.tensor.matmul(out=spread[:], lhsT=ones[:], rhs=bias_row[:, cols], start=True, stop=True)
             nc.scalar.copy(out=bias_all[:, cols], in_=spread[:])
-        quantise(1)
-        products(0)
+        quantise(0, operands=(0,))
+        quantise(0, operands=(1,))
+        products(0, [(half, group) for pair in ((0, 1), (2, 3)) for half in range(HALVES) for group in pair])
+        add_bias(0)
+        sigmoid(0)
+        flip(1)
         candidate(0)
+        candidate(1)
+        quantise(1)
+        difference(0)
+        scale(0)
         flip(2)
+        products(1)
+        difference(1)
+        quantise(2)
+        flip(3)
 
-        for j in range(ROW_TILES):
+        for j in range(1, ROW_TILES):
             add_bias(j)
             sigmoid(j)
             if j + 2 < ROW_TILES:
@@ -205,10 +220,7 @@ def tile_grulrcell_pb_kernel(
                 products(j + 1)
             if j + 3 < ROW_TILES:
                 flip(j + 3)
-            if j >= 1:
-                finish(j - 1)
-            if j == 0:
-                difference(0)
+            finish(j - 1)
             if j + 1 < ROW_TILES:
                 difference(j + 1)
             scale(j)

@@ -23,6 +23,7 @@ PASSES = FEATURES // K_PASS
 GROUPS = 2 * PASSES
 N_HALF = 512
 HALVES = HIDDEN // N_HALF
+DIFF_SPLIT = 768
 
 FLOPS = 2 * ROWS * (2 * FEATURES) * HIDDEN
 
@@ -57,8 +58,9 @@ def tile_grulrcell_pb_kernel(
         ident_bf = keep.tile([P, P], BF16)
         table_warm = keep.tile([P, 1], F32)
 
+        nc.vector.memset(bias_row[:].bitcast(I32), 0)
+        nc.scalar.dma_start(out=bias_row[0:1, :], in_=bias_gate[:, :])
         nc.vector.memset(w_scales[:].rearrange("p k n -> p (k n)").bitcast(I32), 0)
-        nc.vector.memset(bias_row[:], 0.0)
         nc.vector.memset(table_warm[:], 0.0)
         nc.vector.memset(ones[:], 1.0)
         make_identity(nc, ident[:])
@@ -83,7 +85,6 @@ def tile_grulrcell_pb_kernel(
                 in_=words.rearrange("g p b -> p g b").bitcast(I32),
             )
 
-        nc.gpsimd.dma_start(out=bias_row[0:1, :], in_=bias_gate[:, :])
         load_rows(inp_sb, inp_rows, 0)
         load_rows(state_sb, state_rows, 0)
         load_scales(W2_scales, 0)
@@ -173,10 +174,14 @@ def tile_grulrcell_pb_kernel(
             for cols in half_cols:
                 nc.scalar.activation(out=gate[j][:, cols], in_=gate[j][:, cols], func=ACT.Sigmoid)
 
-        def difference(j):
+        def difference_tail(j):
             diff[j] = work.tile([P, HIDDEN], F32, name="diff")
-            for cols in half_cols:
-                nc.vector.tensor_tensor(out=diff[j][:, cols], in0=state_sb[:, j, cols], in1=cand[j][:, cols], op=ALU.subtract)
+            cols = slice(DIFF_SPLIT, HIDDEN)
+            nc.gpsimd.tensor_tensor(out=diff[j][:, cols], in0=state_sb[:, j, cols], in1=c_sb[:, j, cols], op=ALU.subtract)
+
+        def difference(j):
+            cols = slice(0, DIFF_SPLIT)
+            nc.vector.tensor_tensor(out=diff[j][:, cols], in0=state_sb[:, j, cols], in1=cand[j][:, cols], op=ALU.subtract)
 
         def scale(j):
             for cols in half_cols:
@@ -198,12 +203,15 @@ def tile_grulrcell_pb_kernel(
         products(0, [(half, group) for pair in ((0, 1), (2, 3)) for half in range(HALVES) for group in pair])
         add_bias(0)
         sigmoid(0)
+        difference_tail(0)
+        difference_tail(1)
         flip(1)
         candidate(0)
         candidate(1)
         quantise(1)
         difference(0)
         scale(0)
+        difference_tail(2)
         flip(2)
         products(1)
         difference(1)
@@ -220,8 +228,12 @@ def tile_grulrcell_pb_kernel(
                 products(j + 1)
             if j + 3 < ROW_TILES:
                 flip(j + 3)
-            finish(j - 1)
+            if j < ROW_TILES - 2:
+                finish(j - 1)
             if j + 1 < ROW_TILES:
                 difference(j + 1)
             scale(j)
-        finish(ROW_TILES - 1)
+            if j + 2 < ROW_TILES:
+                difference_tail(j + 2)
+        for j in range(ROW_TILES - 3, ROW_TILES):
+            finish(j)

@@ -23,7 +23,8 @@ PASSES = FEATURES // K_PASS
 GROUPS = 2 * PASSES
 N_HALF = 512
 HALVES = HIDDEN // N_HALF
-DIFF_SPLIT = 768
+DIFF_SPLIT = 896
+SORT_FROM = 4
 
 FLOPS = 2 * ROWS * (2 * FEATURES) * HIDDEN
 
@@ -103,6 +104,7 @@ def tile_grulrcell_pb_kernel(
             load_rows(c_sb, c_rows, j - 1)
         load_rows(c_sb, c_rows, ROW_TILES - 1)
 
+        in_order = {}
         grouped = {}
         codes = {}
         code_scales = {}
@@ -111,16 +113,24 @@ def tile_grulrcell_pb_kernel(
         gate = {}
         diff = {}
 
+        def sort_words(j):
+            in_order[j, 1] = work.tile([P, PASSES, 2, P], F32, name="in_order")
+            nc.scalar.copy(
+                out=in_order[j, 1][:],
+                in_=state_sb[:, j, :].bitcast(F32).rearrange("p (g w u) -> p g u w", g=PASSES, u=2),
+            )
+
         def flip(j):
             grouped[j] = work.tile([P, 2, PASSES, P, 4], BF16, name="grouped", align_bytes=64)
             for operand, rows_sb in enumerate((inp_sb, state_sb)):
                 words = rows_sb[:, j, :].bitcast(F32)
+                sorted_words = in_order.get((j, operand))
                 flipped = psum_t.tile([P, PASSES, 2, P], F32, tag="flipped%d" % operand)
                 for g in range(PASSES):
                     for u in range(2):
                         nc.tensor.transpose(
                             flipped[:, g, u, :],
-                            words[:, 256 * g + u : 256 * (g + 1) : 2],
+                            words[:, 256 * g + u : 256 * (g + 1) : 2] if sorted_words is None else sorted_words[:, g, u, :],
                             ident[:],
                         )
                 copy = nc.vector.tensor_copy if operand == 1 and j < 2 else nc.scalar.copy
@@ -202,16 +212,15 @@ def tile_grulrcell_pb_kernel(
         quantise(0, operands=(1,))
         products(0, [(half, group) for pair in ((0, 1), (2, 3)) for half in range(HALVES) for group in pair])
         add_bias(0)
-        sigmoid(0)
-        difference_tail(0)
-        difference_tail(1)
         flip(1)
+        sigmoid(0)
+        for j in range(3):
+            difference_tail(j)
         candidate(0)
         candidate(1)
         quantise(1)
         difference(0)
         scale(0)
-        difference_tail(2)
         flip(2)
         products(1)
         difference(1)
@@ -221,6 +230,8 @@ def tile_grulrcell_pb_kernel(
         for j in range(1, ROW_TILES):
             add_bias(j)
             sigmoid(j)
+            if SORT_FROM <= j + 3 < ROW_TILES:
+                sort_words(j + 3)
             if j + 2 < ROW_TILES:
                 quantise(j + 2)
             if j + 1 < ROW_TILES:

@@ -18,6 +18,7 @@ ROWS = 1024
 FEATURES = 1024
 HIDDEN = 1024
 ROW_TILES = ROWS // P
+LAST = ROW_TILES - 1
 K_PASS = 512
 PASSES = FEATURES // K_PASS
 GROUPS = 2 * PASSES
@@ -57,6 +58,7 @@ def tile_grulrcell_pb_kernel(
         ones = keep.tile([P, P], BF16)
         ident = keep.tile([P, P], F32)
         ident_bf = keep.tile([P, P], BF16)
+        minus_ident = keep.tile([P, P], BF16)
         table_warm = keep.tile([P, 1], F32)
 
         nc.vector.memset(bias_row[:].bitcast(I32), 0)
@@ -66,6 +68,7 @@ def tile_grulrcell_pb_kernel(
         nc.vector.memset(ones[:], 1.0)
         make_identity(nc, ident[:])
         make_identity(nc, ident_bf[:])
+        nc.vector.tensor_scalar(out=minus_ident[:], in0=ident_bf[:], scalar1=-1.0, scalar2=None, op0=ALU.mult)
         nc.scalar.activation(out=table_warm[:], in_=table_warm[:], func=ACT.Sigmoid)
 
         def load_rows(dst, src, j):
@@ -112,6 +115,7 @@ def tile_grulrcell_pb_kernel(
         cand = {}
         gate = {}
         diff = {}
+        result = {}
 
         def sort_words(j):
             in_order[j, 1] = work.tile([P, PASSES, 2, P], F32, name="in_order")
@@ -120,9 +124,11 @@ def tile_grulrcell_pb_kernel(
                 in_=state_sb[:, j, :].bitcast(F32).rearrange("p (g w u) -> p g u w", g=PASSES, u=2),
             )
 
-        def flip(j):
-            grouped[j] = work.tile([P, 2, PASSES, P, 4], BF16, name="grouped", align_bytes=64)
-            for operand, rows_sb in enumerate((inp_sb, state_sb)):
+        def flip(j, operands=(0, 1)):
+            if operands[0] == 0:
+                grouped[j] = work.tile([P, 2, PASSES, P, 4], BF16, name="grouped", align_bytes=64)
+            for operand in operands:
+                rows_sb = (inp_sb, state_sb)[operand]
                 words = rows_sb[:, j, :].bitcast(F32)
                 sorted_words = in_order.get((j, operand))
                 flipped = psum_t.tile([P, PASSES, 2, P], F32, tag="flipped%d" % operand)
@@ -154,7 +160,10 @@ def tile_grulrcell_pb_kernel(
             )
 
         def products(j, order=None):
-            sums[j] = [psum_v.tile([P, N_HALF], F32, name="sums") for half in range(HALVES)]
+            if j == LAST:
+                sums[j] = [psum_t.tile([P, N_HALF], F32, name="sums", tag="flipped%d" % half) for half in range(HALVES)]
+            else:
+                sums[j] = [psum_v.tile([P, N_HALF], F32, name="sums") for half in range(HALVES)]
             for half, group in order or [(half, group) for half in range(HALVES) for group in range(GROUPS)]:
                 rows = slice(group * P, (group + 1) * P)
                 nc.tensor.matmul_mx(
@@ -193,22 +202,35 @@ def tile_grulrcell_pb_kernel(
             cols = slice(0, DIFF_SPLIT)
             nc.vector.tensor_tensor(out=diff[j][:, cols], in0=state_sb[:, j, cols], in1=cand[j][:, cols], op=ALU.subtract)
 
+        def difference_in_psum(j):
+            diff[j] = [
+                psum_c.tile([P, N_HALF], F32, name="last_diff", tag="cand"),
+                psum_v.tile([P, N_HALF], F32, name="last_diff", tag="sums"),
+            ]
+            for half, cols in enumerate(half_cols):
+                nc.tensor.matmul(out=diff[j][half][:], lhsT=ident_bf[:], rhs=state_sb[:, j, cols], start=True, stop=False)
+                nc.tensor.matmul(out=diff[j][half][:], lhsT=minus_ident[:], rhs=c_sb[:, j, cols], start=False, stop=True)
+
         def scale(j):
             for cols in half_cols:
                 nc.gpsimd.tensor_tensor(out=diff[j][:, cols], in0=gate[j][:, cols], in1=diff[j][:, cols], op=ALU.mult)
 
-        def finish(j):
-            result = work.tile([P, HIDDEN], F32)
-            for cols in half_cols:
-                nc.vector.tensor_tensor(out=result[:, cols], in0=diff[j][:, cols], in1=cand[j][:, cols], op=ALU.add)
-                nc.sync.dma_start(out=out_rows[:, j, cols], in_=result[:, cols])
+        def finish(j, halves=range(HALVES)):
+            if j not in result:
+                result[j] = work.tile([P, HIDDEN], F32, name="result")
+            for half in halves:
+                cols = half_cols[half]
+                scaled, candidates = (gate, c_sb[:, j, :]) if j == LAST else (diff, cand[j])
+                nc.vector.tensor_tensor(out=result[j][:, cols], in0=scaled[j][:, cols], in1=candidates[:, cols], op=ALU.add)
+                nc.sync.dma_start(out=out_rows[:, j, cols], in_=result[j][:, cols])
 
-        flip(0)
+        flip(0, operands=(0,))
+        quantise(0, operands=(0,))
+        flip(0, operands=(1,))
         for cols in half_cols:
-            spread = psum_v.tile([P, N_HALF], F32, tag="sums")
+            spread = psum_c.tile([P, N_HALF], F32, tag="cand")
             nc.tensor.matmul(out=spread[:], lhsT=ones[:], rhs=bias_row[:, cols], start=True, stop=True)
             nc.scalar.copy(out=bias_all[:, cols], in_=spread[:])
-        quantise(0, operands=(0,))
         quantise(0, operands=(1,))
         products(0, [(half, group) for pair in ((0, 1), (2, 3)) for half in range(HALVES) for group in pair])
         add_bias(0)
@@ -227,24 +249,28 @@ def tile_grulrcell_pb_kernel(
         quantise(2)
         flip(3)
 
-        for j in range(1, ROW_TILES):
+        for j in range(1, LAST):
             add_bias(j)
             sigmoid(j)
             if SORT_FROM <= j + 3 < ROW_TILES:
                 sort_words(j + 3)
             if j + 2 < ROW_TILES:
                 quantise(j + 2)
-            if j + 1 < ROW_TILES:
+            if j + 1 < LAST:
                 candidate(j + 1)
-                products(j + 1)
+            products(j + 1)
             if j + 3 < ROW_TILES:
                 flip(j + 3)
-            if j < ROW_TILES - 2:
-                finish(j - 1)
-            if j + 1 < ROW_TILES:
+            finish(j - 1)
+            if j + 1 < LAST:
                 difference(j + 1)
             scale(j)
-            if j + 2 < ROW_TILES:
+            if j + 2 < LAST:
                 difference_tail(j + 2)
-        for j in range(ROW_TILES - 3, ROW_TILES):
-            finish(j)
+        difference_in_psum(LAST)
+        add_bias(LAST)
+        sigmoid(LAST)
+        for half, cols in enumerate(half_cols):
+            finish(LAST - 1, [half])
+            nc.vector.tensor_tensor(out=gate[LAST][:, cols], in0=gate[LAST][:, cols], in1=diff[LAST][half][:], op=ALU.mult)
+        finish(LAST)

@@ -19,6 +19,7 @@ FEATURES = 1024
 HIDDEN = 1024
 ROW_TILES = ROWS // P
 LAST = ROW_TILES - 1
+IN_PSUM_FROM = ROW_TILES - 2
 K_PASS = 512
 PASSES = FEATURES // K_PASS
 GROUPS = 2 * PASSES
@@ -184,9 +185,11 @@ def tile_grulrcell_pb_kernel(
 
         half_cols = [slice(half * N_HALF, (half + 1) * N_HALF) for half in range(HALVES)]
 
-        def add_bias(j):
-            gate[j] = work.tile([P, HIDDEN], F32, name="gate")
-            for half, cols in enumerate(half_cols):
+        def add_bias(j, halves=range(HALVES)):
+            if j not in gate:
+                gate[j] = work.tile([P, HIDDEN], F32, name="gate")
+            for half in halves:
+                cols = half_cols[half]
                 nc.vector.tensor_tensor(out=gate[j][:, cols], in0=sums[j][half][:], in1=bias_all[:, cols], op=ALU.add)
 
         def sigmoid(j):
@@ -203,13 +206,15 @@ def tile_grulrcell_pb_kernel(
             nc.vector.tensor_tensor(out=diff[j][:, cols], in0=state_sb[:, j, cols], in1=cand[j][:, cols], op=ALU.subtract)
 
         def difference_in_psum(j):
-            diff[j] = [
-                psum_c.tile([P, N_HALF], F32, name="last_diff", tag="cand"),
-                psum_v.tile([P, N_HALF], F32, name="last_diff", tag="sums"),
-            ]
+            pool, tag = (psum_v, "sums") if j == LAST else (psum_c, "cand")
+            diff[j] = [pool.tile([P, N_HALF], F32, name="diff_psum", tag=tag) for half in range(HALVES)]
             for half, cols in enumerate(half_cols):
                 nc.tensor.matmul(out=diff[j][half][:], lhsT=ident_bf[:], rhs=state_sb[:, j, cols], start=True, stop=False)
                 nc.tensor.matmul(out=diff[j][half][:], lhsT=minus_ident[:], rhs=c_sb[:, j, cols], start=False, stop=True)
+
+        def scale_in_place(j, half):
+            cols = half_cols[half]
+            nc.vector.tensor_tensor(out=gate[j][:, cols], in0=gate[j][:, cols], in1=diff[j][half][:], op=ALU.mult)
 
         def scale(j):
             for cols in half_cols:
@@ -220,8 +225,9 @@ def tile_grulrcell_pb_kernel(
                 result[j] = work.tile([P, HIDDEN], F32, name="result")
             for half in halves:
                 cols = half_cols[half]
-                scaled, candidates = (gate, c_sb[:, j, :]) if j == LAST else (diff, cand[j])
-                nc.vector.tensor_tensor(out=result[j][:, cols], in0=scaled[j][:, cols], in1=candidates[:, cols], op=ALU.add)
+                scaled, candidates = (gate, c_sb[:, j, :]) if j >= IN_PSUM_FROM else (diff, cand[j])
+                engine = nc.gpsimd if IN_PSUM_FROM <= j < LAST else nc.vector
+                engine.tensor_tensor(out=result[j][:, cols], in0=scaled[j][:, cols], in1=candidates[:, cols], op=ALU.add)
                 nc.sync.dma_start(out=out_rows[:, j, cols], in_=result[j][:, cols])
 
         flip(0, operands=(0,))
@@ -249,28 +255,36 @@ def tile_grulrcell_pb_kernel(
         quantise(2)
         flip(3)
 
-        for j in range(1, LAST):
+        for j in range(1, IN_PSUM_FROM):
             add_bias(j)
             sigmoid(j)
             if SORT_FROM <= j + 3 < ROW_TILES:
                 sort_words(j + 3)
             if j + 2 < ROW_TILES:
                 quantise(j + 2)
-            if j + 1 < LAST:
+            if j + 1 < IN_PSUM_FROM:
                 candidate(j + 1)
             products(j + 1)
             if j + 3 < ROW_TILES:
                 flip(j + 3)
             finish(j - 1)
-            if j + 1 < LAST:
+            if j + 1 < IN_PSUM_FROM:
                 difference(j + 1)
             scale(j)
-            if j + 2 < LAST:
+            if j + 2 < IN_PSUM_FROM:
                 difference_tail(j + 2)
+        j = IN_PSUM_FROM
+        add_bias(j)
+        sigmoid(j)
+        difference_in_psum(j)
+        products(LAST)
         difference_in_psum(LAST)
-        add_bias(LAST)
+        for half in range(HALVES):
+            finish(j - 1, [half])
+            scale_in_place(j, half)
+            add_bias(LAST, [half])
+        finish(j)
         sigmoid(LAST)
-        for half, cols in enumerate(half_cols):
-            finish(LAST - 1, [half])
-            nc.vector.tensor_tensor(out=gate[LAST][:, cols], in0=gate[LAST][:, cols], in1=diff[LAST][half][:], op=ALU.mult)
+        for half in range(HALVES):
+            scale_in_place(LAST, half)
         finish(LAST)

@@ -197,11 +197,14 @@ def tile_grulrcell_pb_kernel(
                 nc.scalar.activation(out=gate[j][:, cols], in_=gate[j][:, cols], func=ACT.Sigmoid)
 
         def difference_tail(j):
-            diff[j] = work.tile([P, HIDDEN], F32, name="diff")
+            if j not in diff:
+                diff[j] = work.tile([P, HIDDEN], F32, name="diff")
             cols = slice(DIFF_SPLIT, HIDDEN)
             nc.gpsimd.tensor_tensor(out=diff[j][:, cols], in0=state_sb[:, j, cols], in1=c_sb[:, j, cols], op=ALU.subtract)
 
         def difference(j):
+            if j not in diff:
+                diff[j] = work.tile([P, HIDDEN], F32, name="diff")
             cols = slice(0, DIFF_SPLIT)
             nc.vector.tensor_tensor(out=diff[j][:, cols], in0=state_sb[:, j, cols], in1=cand[j][:, cols], op=ALU.subtract)
 
@@ -242,7 +245,7 @@ def tile_grulrcell_pb_kernel(
         add_bias(0)
         flip(1)
         sigmoid(0)
-        for j in range(3):
+        for j in range(2):
             difference_tail(j)
         candidate(0)
         candidate(1)
@@ -252,7 +255,6 @@ def tile_grulrcell_pb_kernel(
         flip(2)
         products(1)
         difference(1)
-        quantise(2)
         flip(3)
 
         for j in range(1, IN_PSUM_FROM):
@@ -260,6 +262,9 @@ def tile_grulrcell_pb_kernel(
             sigmoid(j)
             if SORT_FROM <= j + 3 < ROW_TILES:
                 sort_words(j + 3)
+            if j == 1:
+                quantise(2)
+            finish(j - 1, [0])
             if j + 2 < ROW_TILES:
                 quantise(j + 2)
             if j + 1 < IN_PSUM_FROM:
@@ -267,10 +272,12 @@ def tile_grulrcell_pb_kernel(
             products(j + 1)
             if j + 3 < ROW_TILES:
                 flip(j + 3)
-            finish(j - 1)
+            finish(j - 1, [1])
             if j + 1 < IN_PSUM_FROM:
                 difference(j + 1)
             scale(j)
+            if j == 1:
+                difference_tail(2)
             if j + 2 < IN_PSUM_FROM:
                 difference_tail(j + 2)
         j = IN_PSUM_FROM

@@ -52,8 +52,8 @@ def tile_grulrcell_pb_kernel(
         inp_sb = keep.tile([P, ROW_TILES, FEATURES], BF16)
         state_sb = keep.tile([P, ROW_TILES, FEATURES], BF16)
         c_sb = keep.tile([P, ROW_TILES, HIDDEN], BF16)
-        w_words = keep.tile([P, GROUPS, 2 * HIDDEN], U8, align_bytes=64)
-        w_scales = keep.tile([P, GROUPS, HIDDEN], U8, align_bytes=64)
+        w_words = keep.tile([P, GROUPS, 2 * HIDDEN], U8, align_bytes=256)
+        w_scales = keep.tile([P, GROUPS, HIDDEN], U8, align_bytes=256)
         bias_row = keep.tile([P, HIDDEN], BF16)
         bias_all = keep.tile([P, HIDDEN], F32)
         ones = keep.tile([P, P], BF16)
@@ -151,8 +151,8 @@ def tile_grulrcell_pb_kernel(
 
         def quantise(j, operands=(0, 1)):
             if operands[0] == 0:
-                codes[j] = work.tile([P, GROUPS * P], U32, name="codes", align_bytes=64)
-                code_scales[j] = work.tile([P, GROUPS * P], U8, name="code_scales", align_bytes=64)
+                codes[j] = work.tile([P, GROUPS * P], U32, name="codes", align_bytes=256)
+                code_scales[j] = work.tile([P, GROUPS * P], U8, name="code_scales", align_bytes=256)
             cols = slice(operands[0] * PASSES * P, (operands[-1] + 1) * PASSES * P)
             nc.vector.quantize_mx(
                 out=codes[j][:, cols].bitcast(FP8X4),
@@ -209,8 +209,10 @@ def tile_grulrcell_pb_kernel(
             nc.vector.tensor_tensor(out=diff[j][:, cols], in0=state_sb[:, j, cols], in1=cand[j][:, cols], op=ALU.subtract)
 
         def difference_in_psum(j):
-            pool, tag = (psum_v, "sums") if j == LAST else (psum_c, "cand")
-            diff[j] = [pool.tile([P, N_HALF], F32, name="diff_psum", tag=tag) for half in range(HALVES)]
+            diff[j] = [
+                psum_c.tile([P, N_HALF], F32, name="diff_psum", tag="cand"),
+                psum_v.tile([P, N_HALF], F32, name="diff_psum", tag="sums"),
+            ]
             for half, cols in enumerate(half_cols):
                 nc.tensor.matmul(out=diff[j][half][:], lhsT=ident_bf[:], rhs=state_sb[:, j, cols], start=True, stop=False)
                 nc.tensor.matmul(out=diff[j][half][:], lhsT=minus_ident[:], rhs=c_sb[:, j, cols], start=False, stop=True)
@@ -226,8 +228,11 @@ def tile_grulrcell_pb_kernel(
         def finish(j, halves=range(HALVES)):
             if j not in result:
                 result[j] = work.tile([P, HIDDEN], F32, name="result")
-            for half in halves:
-                cols = half_cols[half]
+            pieces = [half_cols[half] for half in halves]
+            if j == LAST:
+                middle = HIDDEN - N_HALF // 2
+                pieces = [half_cols[0], slice(N_HALF, middle), slice(middle, HIDDEN)]
+            for cols in pieces:
                 scaled, candidates = (gate, c_sb[:, j, :]) if j >= IN_PSUM_FROM else (diff, cand[j])
                 engine = nc.gpsimd if IN_PSUM_FROM <= j < LAST else nc.vector
                 engine.tensor_tensor(out=result[j][:, cols], in0=scaled[j][:, cols], in1=candidates[:, cols], op=ALU.add)

from contextlib import ExitStack

import concourse.mybir as mybir
from concourse.masks import make_identity

F32 = mybir.dt.float32
BF16 = mybir.dt.bfloat16
I32 = mybir.dt.int32
U32 = mybir.dt.uint32
U8 = mybir.dt.uint8
FP8X4 = mybir.dt.float8_e4m3fn_x4
FP4X4 = mybir.dt.float4_e2m1fn_x4
ALU = mybir.AluOpType
ACT = mybir.ActivationFunctionType

P = 128
ROWS = 1024
FEATURES = 1024
HIDDEN = 1024
ROW_TILES = ROWS // P
LAST = ROW_TILES - 1
IN_PSUM_FROM = ROW_TILES - 2
K_PASS = 512
PASSES = FEATURES // K_PASS
GROUPS = 2 * PASSES
N_HALF = 512
HALVES = HIDDEN // N_HALF
DIFF_SPLIT = 896
SORT_FROM = 4

FLOPS = 2 * ROWS * (2 * FEATURES) * HIDDEN


def tile_grulrcell_pb_kernel(
    tc, inp, state, c, W2_words, W2_scales, U2_words, U2_scales, bias_gate, out
):
    nc = tc.nc

    inp_rows = inp.rearrange("(p j) k -> p j k", j=ROW_TILES)
    state_rows = state.rearrange("(p j) k -> p j k", j=ROW_TILES)
    c_rows = c.rearrange("(p j) h -> p j h", j=ROW_TILES)
    out_rows = out.rearrange("(p j) h -> p j h", j=ROW_TILES)

    with ExitStack() as stack:
        keep = stack.enter_context(tc.tile_pool(name="keep", bufs=1))
        work = stack.enter_context(tc.tile_pool(name="work", bufs=4))
        psum_t = stack.enter_context(tc.psum_pool(name="psum_t", bufs=1))
        psum_v = stack.enter_context(tc.psum_pool(name="psum_v", bufs=3))
        psum_c = stack.enter_context(tc.psum_pool(name="psum_c", bufs=3))
        stack.enter_context(tc.manual_schedule())

        inp_sb = keep.tile([P, ROW_TILES, FEATURES], BF16)
        state_sb = keep.tile([P, ROW_TILES, FEATURES], BF16)
        c_sb = keep.tile([P, ROW_TILES, HIDDEN], BF16)
        w_words = keep.tile([P, GROUPS, 2 * HIDDEN], U8, align_bytes=256)
        w_scales = keep.tile([P, GROUPS, HIDDEN], U8, align_bytes=256)
        bias_row = keep.tile([P, HIDDEN], BF16)
        bias_all = keep.tile([P, HIDDEN], F32)
        ones = keep.tile([P, P], BF16)
        ident = keep.tile([P, P], F32)
        ident_bf = keep.tile([P, P], BF16)
        minus_ident = keep.tile([P, P], BF16)
        table_warm = keep.tile([P, 1], F32)

        nc.vector.memset(bias_row[:].bitcast(I32), 0)
        nc.scalar.dma_start(out=bias_row[0:1, :], in_=bias_gate[:, :])
        nc.vector.memset(w_scales[:].rearrange("p k n -> p (k n)").bitcast(I32), 0)
        nc.vector.memset(table_warm[:], 0.0)
        nc.vector.memset(ones[:], 1.0)
        make_identity(nc, ident[:])
        make_identity(nc, ident_bf[:])
        nc.vector.tensor_scalar(out=minus_ident[:], in0=ident_bf[:], scalar1=-1.0, scalar2=None, op0=ALU.mult)
        nc.scalar.activation(out=table_warm[:], in_=table_warm[:], func=ACT.Sigmoid)

        def load_rows(dst, src, j):
            nc.sync.dma_start(out=dst[:, j, :], in_=src[:, j, :])

        def load_scales(scales, first_group):
            groups = slice(first_group, first_group + PASSES)
            for quad in range(4):
                nc.sync.dma_start(
                    out=w_scales[32 * quad : 32 * quad + 4, groups, :].bitcast(I32),
                    in_=scales[:, 4 * quad : 4 * quad + 4, :].rearrange("g r n -> r g n").bitcast(I32),
                )

        def load_words(words, first_group):
            groups = slice(first_group, first_group + PASSES)
            nc.sync.dma_start(
                out=w_words[:, groups, :].bitcast(I32),
                in_=words.rearrange("g p b -> p g b").bitcast(I32),
            )

        load_rows(inp_sb, inp_rows, 0)
        load_rows(state_sb, state_rows, 0)
        load_scales(W2_scales, 0)
        load_words(W2_words, 0)
        load_words(U2_words, PASSES)
        load_scales(U2_scales, PASSES)
        load_rows(inp_sb, inp_rows, 1)
        load_rows(state_sb, state_rows, 1)
        load_rows(c_sb, c_rows, 0)
        load_rows(c_sb, c_rows, 1)
        load_rows(inp_sb, inp_rows, 2)
        load_rows(state_sb, state_rows, 2)
        for j in range(3, ROW_TILES):
            load_rows(inp_sb, inp_rows, j)
            load_rows(state_sb, state_rows, j)
            load_rows(c_sb, c_rows, j - 1)
        load_rows(c_sb, c_rows, ROW_TILES - 1)

        in_order = {}
        grouped = {}
        codes = {}
        code_scales = {}
        sums = {}
        cand = {}
        gate = {}
        diff = {}
        result = {}

        def sort_words(j):
            in_order[j, 1] = work.tile([P, PASSES, 2, P], F32, name="in_order")
            nc.scalar.copy(
                out=in_order[j, 1][:],
                in_=state_sb[:, j, :].bitcast(F32).rearrange("p (g w u) -> p g u w", g=PASSES, u=2),
            )

        def flip(j, operands=(0, 1)):
            if operands[0] == 0:
                grouped[j] = work.tile([P, 2, PASSES, P, 4], BF16, name="grouped", align_bytes=64)
            for operand in operands:
                rows_sb = (inp_sb, state_sb)[operand]
                words = rows_sb[:, j, :].bitcast(F32)
                sorted_words = in_order.get((j, operand))
                flipped = psum_t.tile([P, PASSES, 2, P], F32, tag="flipped%d" % operand)
                for g in range(PASSES):
                    for u in range(2):
                        nc.tensor.transpose(
                            flipped[:, g, u, :],
                            words[:, 256 * g + u : 256 * (g + 1) : 2] if sorted_words is None else sorted_words[:, g, u, :],
                            ident[:],
                        )
                copy = nc.vector.tensor_copy if operand == 1 and j < 2 else nc.scalar.copy
                copy(
                    out=grouped[j][:, operand]
                    .rearrange("p g r t -> p (g r t)")
                    .bitcast(F32)
                    .rearrange("p (g r u) -> p g r u", g=PASSES, u=2),
                    in_=flipped[:].rearrange("p g u r -> p g r u"),
                )

        def quantise(j, operands=(0, 1)):
            if operands[0] == 0:
                codes[j] = work.tile([P, GROUPS * P], U32, name="codes", align_bytes=256)
                code_scales[j] = work.tile([P, GROUPS * P], U8, name="code_scales", align_bytes=256)
            cols = slice(operands[0] * PASSES * P, (operands[-1] + 1) * PASSES * P)
            nc.vector.quantize_mx(
                out=codes[j][:, cols].bitcast(FP8X4),
                scales=code_scales[j][:, cols],
                in_=grouped[j][:, operands[0] : operands[-1] + 1].rearrange("p o g r t -> p (o g r t)"),
            )

        def products(j, order=None):
            if j == LAST:
                sums[j] = [psum_t.tile([P, N_HALF], F32, name="sums", tag="flipped%d" % half) for half in range(HALVES)]
            else:
                sums[j] = [psum_v.tile([P, N_HALF], F32, name="sums") for half in range(HALVES)]
            for half, group in order or [(half, group) for half in range(HALVES) for group in range(GROUPS)]:
                rows = slice(group * P, (group + 1) * P)
                nc.tensor.matmul_mx(
                    out=sums[j][half][:],
                    lhsT=codes[j][:, rows].bitcast(FP8X4),
                    lhsT_scale=code_scales[j][:, rows],
                    rhs=w_words[:, group, 2 * half * N_HALF : 2 * (half + 1) * N_HALF].bitcast(FP4X4),
                    rhs_scale=w_scales[:, group, half * N_HALF : (half + 1) * N_HALF],
                    start=(group == 0),
                    stop=(group == GROUPS - 1),
                )

        def candidate(j):
            cand[j] = psum_c.tile([P, HIDDEN], BF16, name="cand")
            for half in range(HALVES):
                cols = slice(half * N_HALF, (half + 1) * N_HALF)
                nc.tensor.matmul(out=cand[j][:, cols], lhsT=ident_bf[:], rhs=c_sb[:, j, cols], start=True, stop=True)

        half_cols = [slice(half * N_HALF, (half + 1) * N_HALF) for half in range(HALVES)]

        def add_bias(j, halves=range(HALVES)):
            if j not in gate:
                gate[j] = work.tile([P, HIDDEN], F32, name="gate")
            for half in halves:
                cols = half_cols[half]
                nc.vector.tensor_tensor(out=gate[j][:, cols], in0=sums[j][half][:], in1=bias_all[:, cols], op=ALU.add)

        def sigmoid(j):
            for cols in half_cols:
                nc.scalar.activation(out=gate[j][:, cols], in_=gate[j][:, cols], func=ACT.Sigmoid)

        def difference_tail(j):
            if j not in diff:
                diff[j] = work.tile([P, HIDDEN], F32, name="diff")
            cols = slice(DIFF_SPLIT, HIDDEN)
            nc.gpsimd.tensor_tensor(out=diff[j][:, cols], in0=state_sb[:, j, cols], in1=c_sb[:, j, cols], op=ALU.subtract)

        def difference(j):
            if j not in diff:
                diff[j] = work.tile([P, HIDDEN], F32, name="diff")
            cols = slice(0, DIFF_SPLIT)
            nc.vector.tensor_tensor(out=diff[j][:, cols], in0=state_sb[:, j, cols], in1=cand[j][:, cols], op=ALU.subtract)

        def difference_in_psum(j):
            diff[j] = [
                psum_c.tile([P, N_HALF], F32, name="diff_psum", tag="cand"),
                psum_v.tile([P, N_HALF], F32, name="diff_psum", tag="sums"),
            ]
            for half, cols in enumerate(half_cols):
                nc.tensor.matmul(out=diff[j][half][:], lhsT=ident_bf[:], rhs=state_sb[:, j, cols], start=True, stop=False)
                nc.tensor.matmul(out=diff[j][half][:], lhsT=minus_ident[:], rhs=c_sb[:, j, cols], start=False, stop=True)

        def scale_in_place(j, half):
            cols = half_cols[half]
            nc.vector.tensor_tensor(out=gate[j][:, cols], in0=gate[j][:, cols], in1=diff[j][half][:], op=ALU.mult)

        def scale(j):
            for cols in half_cols:
                nc.gpsimd.tensor_tensor(out=diff[j][:, cols], in0=gate[j][:, cols], in1=diff[j][:, cols], op=ALU.mult)

        def finish(j, halves=range(HALVES)):
            if j not in result:
                result[j] = work.tile([P, HIDDEN], F32, name="result")
            pieces = [half_cols[half] for half in halves]
            if j == LAST:
                middle = HIDDEN - N_HALF // 2
                pieces = [half_cols[0], slice(N_HALF, middle), slice(middle, HIDDEN)]
            for cols in pieces:
                scaled, candidates = (gate, c_sb[:, j, :]) if j >= IN_PSUM_FROM else (diff, cand[j])
                engine = nc.gpsimd if IN_PSUM_FROM <= j < LAST else nc.vector
                engine.tensor_tensor(out=result[j][:, cols], in0=scaled[j][:, cols], in1=candidates[:, cols], op=ALU.add)
                nc.sync.dma_start(out=out_rows[:, j, cols], in_=result[j][:, cols])

        flip(0, operands=(0,))
        quantise(0, operands=(0,))
        flip(0, operands=(1,))
        for cols in half_cols:
            spread = psum_c.tile([P, N_HALF], F32, tag="cand")
            nc.tensor.matmul(out=spread[:], lhsT=ones[:], rhs=bias_row[:, cols], start=True, stop=True)
            nc.scalar.copy(out=bias_all[:, cols], in_=spread[:])
        quantise(0, operands=(1,))
        products(0, [(half, group) for pair in ((0, 1), (2, 3)) for half in range(HALVES) for group in pair])
        add_bias(0)
        flip(1)
        sigmoid(0)
        for j in range(2):
            difference_tail(j)
        candidate(0)
        candidate(1)
        quantise(1)
        difference(0)
        scale(0)
        flip(2)
        products(1)
        difference(1)
        flip(3)

        for j in range(1, IN_PSUM_FROM):
            add_bias(j)
            sigmoid(j)
            if SORT_FROM <= j + 3 < ROW_TILES:
                sort_words(j + 3)
            if j == 1:
                quantise(2)
            finish(j - 1, [0])
            if j + 2 < ROW_TILES:
                quantise(j + 2)
            if j + 1 < IN_PSUM_FROM:
                candidate(j + 1)
            products(j + 1)
            if j + 3 < ROW_TILES:
                flip(j + 3)
            finish(j - 1, [1])
            if j + 1 < IN_PSUM_FROM:
                difference(j + 1)
            scale(j)
            if j == 1:
                difference_tail(2)
            if j + 2 < IN_PSUM_FROM:
                difference_tail(j + 2)
        j = IN_PSUM_FROM
        add_bias(j)
        sigmoid(j)
        difference_in_psum(j)
        products(LAST)
        difference_in_psum(LAST)
        for half in range(HALVES):
            finish(j - 1, [half])
            scale_in_place(j, half)
            add_bias(LAST, [half])
        finish(j)
        sigmoid(LAST)
        for half in range(HALVES):
            scale_in_place(LAST, half)
        finish(LAST)
